import numpy as np
import ml_dtypes

BF16 = ml_dtypes.bfloat16


def bf(x):
    return np.asarray(x, np.float32).astype(BF16)


def f32(x):
    return np.asarray(x, np.float32)


def f64(x):
    return np.asarray(x).astype(np.float64)


def striped(idx):
    return np.tile(idx.reshape(-1, 16).T, (8, 1))


D, S, N, HID, Q, H, K = 128, 512, 4096, 512, 4, 256, 16


def setup_inputs():
    return {"h": f32(np.random.standard_normal((D, S))), "hi": f32(np.random.standard_normal((D, N))), "w1": bf(np.random.standard_normal((Q * D, HID)) / np.sqrt(Q * D)), "b1": f32(0.1 * np.random.standard_normal((HID, 1))), "w2": bf(np.random.standard_normal((HID, HID)) / np.sqrt(HID)), "b2": f32(0.1 * np.random.standard_normal((HID, 1))), "offs": striped(np.concatenate([np.random.permutation(S)[:H] for _ in range(K)]))}


def reference(h, hi, w1, b1, w2, b2, offs):
    idx = offs[:16].T.reshape(-1)
    wa, wb, wc, wd = f64(w1).reshape(Q, D, HID)
    first = f64(hi)
    picked = f64(h)[:, idx]
    d = picked + (-first)
    p = picked * first
    x1 = np.maximum(wa.T @ first + wb.T @ picked + wc.T @ np.abs(d) + wd.T @ p + f64(b1), 0.0)
    return np.maximum(f64(w2).T @ x1 + f64(b2), 0.0)

@@ -1,0 +1,98 @@
+import concourse.masks as masks
+import concourse.mybir as mybir
+
+F32, BF16, U16 = mybir.dt.float32, mybir.dt.bfloat16, mybir.dt.uint16
+ADD, MULT, MAX = mybir.AluOpType.add, mybir.AluOpType.mult, mybir.AluOpType.max
+COPY, RELU = mybir.ActivationFunctionType.Copy, mybir.ActivationFunctionType.Relu
+
+P = 128
+NODES = 512
+EDGES = 4096
+HID = 512
+BLOCKS = HID // P
+CHUNK = 512
+N_CHUNKS = EDGES // CHUNK
+
+FLOPS = 2 * EDGES * (BLOCKS * P * HID + HID * HID)
+
+
+def tile_stochasticrewiring_b_kernel(tc, h, hi, w1, b1, w2, b2, offs, out):
+    nc = tc.nc
+    with (
+        tc.tile_pool(name="held", bufs=1) as held,
+        tc.tile_pool(name="work", bufs=2) as work,
+        tc.tile_pool(name="feat", bufs=2) as feat,
+        tc.tile_pool(name="hidden", bufs=2) as hidden,
+        tc.tile_pool(name="staged", bufs=4) as staged,
+    ):
+        offsets = held.tile([P, EDGES // 16], U16, name="offsets")
+        nc.sync.dma_start(offsets[:], offs)
+        h_sb = held.tile([P, NODES], F32, name="h_sb")
+        nc.sync.dma_start(h_sb[:], h)
+        hi_sb = [held.tile([P, CHUNK], F32, name=f"hi_sb{c}") for c in range(N_CHUNKS)]
+        for c in range(N_CHUNKS):
+            nc.sync.dma_start(hi_sb[c][:], hi[:, c * CHUNK : (c + 1) * CHUNK])
+
+        w1_sb = held.tile([P, BLOCKS, HID], BF16, name="w1_sb")
+        nc.scalar.dma_start(w1_sb[:], w1.rearrange("(k p) m -> p k m", p=P))
+        bias_rows = held.tile([P, P], F32, name="bias_rows")
+        nc.vector.memset(bias_rows[:], 0.0)
+        nc.scalar.dma_start(bias_rows[0:BLOCKS, :], b1.rearrange("(m p) o -> m (p o)", p=P))
+        nc.scalar.dma_start(bias_rows[BLOCKS : 2 * BLOCKS, :], b2.rearrange("(m p) o -> m (p o)", p=P))
+        w2_sb = held.tile([P, BLOCKS, HID], BF16, name="w2_sb")
+        nc.scalar.dma_start(w2_sb[:], w2.rearrange("(k p) m -> p k m", p=P))
+
+        identity = held.tile([P, P], F32, name="identity")
+        masks.make_identity(nc, identity[:])
+        bias = held.tile([P, 2 * BLOCKS], F32, name="bias")
+        with tc.psum_pool(name="setup", bufs=1) as setup:
+            bias_cols = setup.tile([P, P], F32, name="bias_cols")
+            nc.tensor.transpose(bias_cols[:], bias_rows[:], identity[:])
+            nc.vector.tensor_copy(bias[:], bias_cols[:, 0 : 2 * BLOCKS])
+
+        def features(c):
+            first = hi_sb[c]
+            picked_cols = h_sb[:].indirect(offsets[:, c * (CHUNK // 16) : (c + 1) * (CHUNK // 16)])
+            neg_first = work.tile([P, CHUNK], F32, name="neg_first")
+            nc.scalar.activation(neg_first[:], first[:], COPY, scale=-1.0)
+            first_bf = feat.tile([P, CHUNK], BF16, name="first_bf")
+            nc.scalar.activation(first_bf[:], first[:], COPY)
+            diff = work.tile([P, CHUNK], F32, name="diff")
+            nc.vector.tensor_tensor(diff[:], picked_cols, neg_first[:], ADD)
+            prod = work.tile([P, CHUNK], F32, name="prod")
+            nc.vector.tensor_tensor(prod[:], picked_cols, first[:], MULT)
+            picked_bf = feat.tile([P, CHUNK], BF16, name="picked_bf")
+            nc.vector.tensor_tensor(picked_bf[:], diff[:], first[:], ADD)
+            absdiff_bf = feat.tile([P, CHUNK], BF16, name="absdiff_bf")
+            nc.vector.scalar_tensor_tensor(absdiff_bf[:], diff[:], -1.0, diff[:], MULT, MAX)
+            prod_bf = feat.tile([P, CHUNK], BF16, name="prod_bf")
+            nc.vector.tensor_copy(prod_bf[:], prod[:])
+            return [first_bf, picked_bf, absdiff_bf, prod_bf]
+
+        with tc.psum_pool(name="psum", bufs=4) as psum:
+            ready = features(0)
+            for c in range(N_CHUNKS):
+                current = ready
+                if c + 1 < N_CHUNKS:
+                    ready = features(c + 1)
+
+                x1 = []
+                for m in range(BLOCKS):
+                    acc1 = psum.tile([P, CHUNK], F32, name="acc1")
+                    for k in range(BLOCKS):
+                        nc.tensor.matmul(
+                            acc1[:], w1_sb[:, k, m * P : (m + 1) * P], current[k][:], start=(k == 0), stop=(k == BLOCKS - 1)
+                        )
+                    x1_m = hidden.tile([P, CHUNK], BF16, name=f"x1_{m}")
+                    nc.scalar.activation(x1_m[:], acc1[:], RELU, bias=bias[:, m : m + 1])
+                    x1.append(x1_m)
+
+                for r in range(BLOCKS):
+                    acc2 = psum.tile([P, CHUNK], F32, name="acc2")
+                    for k in range(BLOCKS):
+                        nc.tensor.matmul(
+                            acc2[:], w2_sb[:, k, r * P : (r + 1) * P], x1[k][:], start=(k == 0), stop=(k == BLOCKS - 1)
+                        )
+                    result = staged.tile([P, CHUNK], F32, name="result")
+                    nc.scalar.activation(result[:], acc2[:], RELU, bias=bias[:, BLOCKS + r : BLOCKS + r + 1])
+                    nc.sync.dma_start(out[r * P : (r + 1) * P, c * CHUNK : (c + 1) * CHUNK], result[:])

@@ -12,6 +12,8 @@ HID = 512
 BLOCKS = HID // P
 CHUNK = 512
 N_CHUNKS = EDGES // CHUNK
+FIRST, PICKED, ABSDIFF, PROD = 0, 1, 2, 3
+READY_ORDER = (FIRST, PROD, ABSDIFF, PICKED)
 
 FLOPS = 2 * EDGES * (BLOCKS * P * HID + HID * HID)
 
@@ -21,7 +23,7 @@ def tile_stochasticrewiring_b_kernel(tc, h, hi, w1, b1, w2, b2, offs, out):
     with (
         tc.tile_pool(name="held", bufs=1) as held,
         tc.tile_pool(name="work", bufs=2) as work,
-        tc.tile_pool(name="feat", bufs=2) as feat,
+        tc.tile_pool(name="feat", bufs=3) as feat,
         tc.tile_pool(name="hidden", bufs=2) as hidden,
         tc.tile_pool(name="staged", bufs=4) as staged,
     ):
@@ -36,7 +38,7 @@ def tile_stochasticrewiring_b_kernel(tc, h, hi, w1, b1, w2, b2, offs, out):
         w1_sb = held.tile([P, BLOCKS, HID], BF16, name="w1_sb")
         nc.scalar.dma_start(w1_sb[:], w1.rearrange("(k p) m -> p k m", p=P))
         bias_rows = held.tile([P, P], F32, name="bias_rows")
-        nc.vector.memset(bias_rows[:], 0.0)
+        nc.gpsimd.memset(bias_rows[:], 0.0)
         nc.scalar.dma_start(bias_rows[0:BLOCKS, :], b1.rearrange("(m p) o -> m (p o)", p=P))
         nc.scalar.dma_start(bias_rows[BLOCKS : 2 * BLOCKS, :], b2.rearrange("(m p) o -> m (p o)", p=P))
         w2_sb = held.tile([P, BLOCKS, HID], BF16, name="w2_sb")
@@ -48,47 +50,48 @@ def tile_stochasticrewiring_b_kernel(tc, h, hi, w1, b1, w2, b2, offs, out):
         with tc.psum_pool(name="setup", bufs=1) as setup:
             bias_cols = setup.tile([P, P], F32, name="bias_cols")
             nc.tensor.transpose(bias_cols[:], bias_rows[:], identity[:])
-            nc.vector.tensor_copy(bias[:], bias_cols[:, 0 : 2 * BLOCKS])
+            nc.scalar.activation(bias[:], bias_cols[:, 0 : 2 * BLOCKS], COPY)
 
         def features(c):
             first = hi_sb[c]
             picked_cols = h_sb[:].indirect(offsets[:, c * (CHUNK // 16) : (c + 1) * (CHUNK // 16)])
-            neg_first = work.tile([P, CHUNK], F32, name="neg_first")
-            nc.scalar.activation(neg_first[:], first[:], COPY, scale=-1.0)
             first_bf = feat.tile([P, CHUNK], BF16, name="first_bf")
             nc.scalar.activation(first_bf[:], first[:], COPY)
-            diff = work.tile([P, CHUNK], F32, name="diff")
-            nc.vector.tensor_tensor(diff[:], picked_cols, neg_first[:], ADD)
+            neg_first = work.tile([P, CHUNK], F32, name="neg_first")
+            nc.scalar.activation(neg_first[:], first[:], COPY, scale=-1.0)
             prod = work.tile([P, CHUNK], F32, name="prod")
             nc.vector.tensor_tensor(prod[:], picked_cols, first[:], MULT)
-            picked_bf = feat.tile([P, CHUNK], BF16, name="picked_bf")
-            nc.vector.tensor_tensor(picked_bf[:], diff[:], first[:], ADD)
-            absdiff_bf = feat.tile([P, CHUNK], BF16, name="absdiff_bf")
-            nc.vector.scalar_tensor_tensor(absdiff_bf[:], diff[:], -1.0, diff[:], MULT, MAX)
             prod_bf = feat.tile([P, CHUNK], BF16, name="prod_bf")
             nc.vector.tensor_copy(prod_bf[:], prod[:])
-            return [first_bf, picked_bf, absdiff_bf, prod_bf]
+            diff = work.tile([P, CHUNK], F32, name="diff")
+            nc.vector.tensor_tensor(diff[:], picked_cols, neg_first[:], ADD)
+            absdiff_bf = feat.tile([P, CHUNK], BF16, name="absdiff_bf")
+            nc.vector.scalar_tensor_tensor(absdiff_bf[:], diff[:], -1.0, diff[:], MULT, MAX)
+            picked_bf = feat.tile([P, CHUNK], BF16, name="picked_bf")
+            nc.vector.tensor_tensor(picked_bf[:], diff[:], first[:], ADD)
+            return {FIRST: first_bf, PICKED: picked_bf, ABSDIFF: absdiff_bf, PROD: prod_bf}
 
-        with tc.psum_pool(name="psum", bufs=4) as psum:
-            ready = features(0)
-            for c in range(N_CHUNKS):
-                current = ready
-                if c + 1 < N_CHUNKS:
-                    ready = features(c + 1)
+        with tc.psum_pool(name="psum1", bufs=1) as psum1, tc.psum_pool(name="psum2", bufs=4) as psum2:
 
-                x1 = []
-                for m in range(BLOCKS):
-                    acc1 = psum.tile([P, CHUNK], F32, name="acc1")
-                    for k in range(BLOCKS):
+            def layer1(feats):
+                acc1 = [psum1.tile([P, CHUNK], F32, name=f"acc1_{m}") for m in range(BLOCKS)]
+                for k in READY_ORDER:
+                    for m in range(BLOCKS):
                         nc.tensor.matmul(
-                            acc1[:], w1_sb[:, k, m * P : (m + 1) * P], current[k][:], start=(k == 0), stop=(k == BLOCKS - 1)
+                            acc1[m][:],
+                            w1_sb[:, k, m * P : (m + 1) * P],
+                            feats[k][:],
+                            start=(k == READY_ORDER[0]),
+                            stop=(k == READY_ORDER[-1]),
                         )
-                    x1_m = hidden.tile([P, CHUNK], BF16, name=f"x1_{m}")
-                    nc.scalar.activation(x1_m[:], acc1[:], RELU, bias=bias[:, m : m + 1])
-                    x1.append(x1_m)
+                x1 = [hidden.tile([P, CHUNK], BF16, name=f"x1_{m}") for m in range(BLOCKS)]
+                for m in range(BLOCKS):
+                    nc.scalar.activation(x1[m][:], acc1[m][:], RELU, bias=bias[:, m : m + 1])
+                return x1
 
+            def layer2(c, x1):
                 for r in range(BLOCKS):
-                    acc2 = psum.tile([P, CHUNK], F32, name="acc2")
+                    acc2 = psum2.tile([P, CHUNK], F32, name="acc2")
                     for k in range(BLOCKS):
                         nc.tensor.matmul(
                             acc2[:], w2_sb[:, k, r * P : (r + 1) * P], x1[k][:], start=(k == 0), stop=(k == BLOCKS - 1)
@@ -96,3 +99,12 @@ def tile_stochasticrewiring_b_kernel(tc, h, hi, w1, b1, w2, b2, offs, out):
                     result = staged.tile([P, CHUNK], F32, name="result")
                     nc.scalar.activation(result[:], acc2[:], RELU, bias=bias[:, BLOCKS + r : BLOCKS + r + 1])
                     nc.sync.dma_start(out[r * P : (r + 1) * P, c * CHUNK : (c + 1) * CHUNK], result[:])
+
+            feats = [features(0), features(1)]
+            x1 = [layer1(feats[0])]
+            for c in range(N_CHUNKS):
+                if c + 2 < N_CHUNKS:
+                    feats.append(features(c + 2))
+                if c + 1 < N_CHUNKS:
+                    x1.append(layer1(feats[c + 1]))
+                layer2(c, x1[c])

@@ -27,30 +27,29 @@ def tile_stochasticrewiring_b_kernel(tc, h, hi, w1, b1, w2, b2, offs, out):
         tc.tile_pool(name="hidden", bufs=2) as hidden,
         tc.tile_pool(name="staged", bufs=4) as staged,
     ):
+        hi_sb = [held.tile([P, CHUNK], F32, name=f"hi_sb{c}") for c in range(N_CHUNKS)]
+        nc.scalar.dma_start(hi_sb[0][:], hi[:, 0:CHUNK])
         offsets = held.tile([P, EDGES // 16], U16, name="offsets")
         nc.sync.dma_start(offsets[:], offs)
         h_sb = held.tile([P, NODES], F32, name="h_sb")
         nc.sync.dma_start(h_sb[:], h)
-        hi_sb = [held.tile([P, CHUNK], F32, name=f"hi_sb{c}") for c in range(N_CHUNKS)]
-        for c in range(N_CHUNKS):
-            nc.sync.dma_start(hi_sb[c][:], hi[:, c * CHUNK : (c + 1) * CHUNK])
-
         w1_sb = held.tile([P, BLOCKS, HID], BF16, name="w1_sb")
-        nc.scalar.dma_start(w1_sb[:], w1.rearrange("(k p) m -> p k m", p=P))
+        w1_blocks = w1.rearrange("(k p) m -> p k m", p=P)
+        nc.sync.dma_start(w1_sb[:, 0:1, :], w1_blocks[:, 0:1, :])
+        nc.sync.dma_start(w1_sb[:, 1:BLOCKS, :], w1_blocks[:, 1:BLOCKS, :])
+        nc.sync.dma_start(hi_sb[1][:], hi[:, CHUNK : 2 * CHUNK])
         bias_rows = held.tile([P, P], F32, name="bias_rows")
         nc.gpsimd.memset(bias_rows[:], 0.0)
-        nc.scalar.dma_start(bias_rows[0:BLOCKS, :], b1.rearrange("(m p) o -> m (p o)", p=P))
-        nc.scalar.dma_start(bias_rows[BLOCKS : 2 * BLOCKS, :], b2.rearrange("(m p) o -> m (p o)", p=P))
+        nc.sync.dma_start(bias_rows[0:BLOCKS, :], b1.rearrange("(m p) o -> m (p o)", p=P))
+        nc.sync.dma_start(bias_rows[BLOCKS : 2 * BLOCKS, :], b2.rearrange("(m p) o -> m (p o)", p=P))
         w2_sb = held.tile([P, BLOCKS, HID], BF16, name="w2_sb")
-        nc.scalar.dma_start(w2_sb[:], w2.rearrange("(k p) m -> p k m", p=P))
+        nc.sync.dma_start(w2_sb[:], w2.rearrange("(k p) m -> p k m", p=P))
+        for c in range(2, N_CHUNKS):
+            nc.sync.dma_start(hi_sb[c][:], hi[:, c * CHUNK : (c + 1) * CHUNK])
 
         identity = held.tile([P, P], F32, name="identity")
         masks.make_identity(nc, identity[:])
         bias = held.tile([P, 2 * BLOCKS], F32, name="bias")
-        with tc.psum_pool(name="setup", bufs=1) as setup:
-            bias_cols = setup.tile([P, P], F32, name="bias_cols")
-            nc.tensor.transpose(bias_cols[:], bias_rows[:], identity[:])
-            nc.scalar.activation(bias[:], bias_cols[:, 0 : 2 * BLOCKS], COPY)
 
         def features(c):
             first = hi_sb[c]
@@ -71,10 +70,10 @@ def tile_stochasticrewiring_b_kernel(tc, h, hi, w1, b1, w2, b2, offs, out):
             nc.vector.tensor_tensor(picked_bf[:], diff[:], first[:], ADD)
             return {FIRST: first_bf, PICKED: picked_bf, ABSDIFF: absdiff_bf, PROD: prod_bf}
 
-        with tc.psum_pool(name="psum1", bufs=1) as psum1, tc.psum_pool(name="psum2", bufs=4) as psum2:
+        with tc.psum_pool(name="psum", bufs=8) as psum:
 
-            def layer1(feats):
-                acc1 = [psum1.tile([P, CHUNK], F32, name=f"acc1_{m}") for m in range(BLOCKS)]
+            def layer1_products(feats):
+                acc1 = [psum.tile([P, CHUNK], F32, name=f"acc1_{m}", tag="acc") for m in range(BLOCKS)]
                 for k in READY_ORDER:
                     for m in range(BLOCKS):
                         nc.tensor.matmul(
@@ -84,6 +83,9 @@ def tile_stochasticrewiring_b_kernel(tc, h, hi, w1, b1, w2, b2, offs, out):
                             start=(k == READY_ORDER[0]),
                             stop=(k == READY_ORDER[-1]),
                         )
+                return acc1
+
+            def layer1_relu(acc1):
                 x1 = [hidden.tile([P, CHUNK], BF16, name=f"x1_{m}") for m in range(BLOCKS)]
                 for m in range(BLOCKS):
                     nc.scalar.activation(x1[m][:], acc1[m][:], RELU, bias=bias[:, m : m + 1])
@@ -91,7 +93,7 @@ def tile_stochasticrewiring_b_kernel(tc, h, hi, w1, b1, w2, b2, offs, out):
 
             def layer2(c, x1):
                 for r in range(BLOCKS):
-                    acc2 = psum2.tile([P, CHUNK], F32, name="acc2")
+                    acc2 = psum.tile([P, CHUNK], F32, name="acc2", tag="acc")
                     for k in range(BLOCKS):
                         nc.tensor.matmul(
                             acc2[:], w2_sb[:, k, r * P : (r + 1) * P], x1[k][:], start=(k == 0), stop=(k == BLOCKS - 1)
@@ -101,10 +103,14 @@ def tile_stochasticrewiring_b_kernel(tc, h, hi, w1, b1, w2, b2, offs, out):
                     nc.sync.dma_start(out[r * P : (r + 1) * P, c * CHUNK : (c + 1) * CHUNK], result[:])
 
             feats = [features(0), features(1)]
-            x1 = [layer1(feats[0])]
+            acc1 = layer1_products(feats[0])
+            bias_cols = psum.tile([P, CHUNK], F32, name="bias_cols", tag="acc")
+            nc.tensor.transpose(bias_cols[:, 0:P], bias_rows[:], identity[:])
+            nc.scalar.activation(bias[:], bias_cols[:, 0 : 2 * BLOCKS], COPY)
+            x1 = [layer1_relu(acc1)]
             for c in range(N_CHUNKS):
                 if c + 2 < N_CHUNKS:
                     feats.append(features(c + 2))
                 if c + 1 < N_CHUNKS:
-                    x1.append(layer1(feats[c + 1]))
+                    x1.append(layer1_relu(layer1_products(feats[c + 1])))
                 layer2(c, x1[c])

@@ -99,7 +99,10 @@ def tile_stochasticrewiring_b_kernel(tc, h, hi, w1, b1, w2, b2, offs, out):
                             acc2[:], w2_sb[:, k, r * P : (r + 1) * P], x1[k][:], start=(k == 0), stop=(k == BLOCKS - 1)
                         )
                     result = staged.tile([P, CHUNK], F32, name="result")
-                    nc.scalar.activation(result[:], acc2[:], RELU, bias=bias[:, BLOCKS + r : BLOCKS + r + 1])
+                    if r % 2 == 0:
+                        nc.scalar.activation(result[:], acc2[:], RELU, bias=bias[:, BLOCKS + r : BLOCKS + r + 1])
+                    else:
+                        nc.vector.tensor_scalar(result[:], acc2[:], bias[:, BLOCKS + r : BLOCKS + r + 1], 0.0, ADD, MAX)
                     nc.sync.dma_start(out[r * P : (r + 1) * P, c * CHUNK : (c + 1) * CHUNK], result[:])
 
             feats = [features(0), features(1)]

@@ -1,4 +1,3 @@
-import concourse.masks as masks
 import concourse.mybir as mybir
 
 F32, BF16, U16 = mybir.dt.float32, mybir.dt.bfloat16, mybir.dt.uint16
@@ -38,18 +37,14 @@ def tile_stochasticrewiring_b_kernel(tc, h, hi, w1, b1, w2, b2, offs, out):
         nc.sync.dma_start(w1_sb[:, 0:1, :], w1_blocks[:, 0:1, :])
         nc.sync.dma_start(w1_sb[:, 1:BLOCKS, :], w1_blocks[:, 1:BLOCKS, :])
         nc.sync.dma_start(hi_sb[1][:], hi[:, CHUNK : 2 * CHUNK])
-        bias_rows = held.tile([P, P], F32, name="bias_rows")
-        nc.gpsimd.memset(bias_rows[:], 0.0)
-        nc.sync.dma_start(bias_rows[0:BLOCKS, :], b1.rearrange("(m p) o -> m (p o)", p=P))
-        nc.sync.dma_start(bias_rows[BLOCKS : 2 * BLOCKS, :], b2.rearrange("(m p) o -> m (p o)", p=P))
+        bias1 = held.tile([P, BLOCKS], F32, name="bias1")
+        nc.sync.dma_start(bias1[:], b1.rearrange("(m p) o -> p (m o)", p=P))
+        bias2 = held.tile([P, BLOCKS], F32, name="bias2")
+        nc.sync.dma_start(bias2[:], b2.rearrange("(m p) o -> p (m o)", p=P))
         w2_sb = held.tile([P, BLOCKS, HID], BF16, name="w2_sb")
         nc.sync.dma_start(w2_sb[:], w2.rearrange("(k p) m -> p k m", p=P))
         for c in range(2, N_CHUNKS):
             nc.sync.dma_start(hi_sb[c][:], hi[:, c * CHUNK : (c + 1) * CHUNK])
-
-        identity = held.tile([P, P], F32, name="identity")
-        masks.make_identity(nc, identity[:])
-        bias = held.tile([P, 2 * BLOCKS], F32, name="bias")
 
         def features(c):
             first = hi_sb[c]
@@ -88,7 +83,7 @@ def tile_stochasticrewiring_b_kernel(tc, h, hi, w1, b1, w2, b2, offs, out):
             def layer1_relu(acc1):
                 x1 = [hidden.tile([P, CHUNK], BF16, name=f"x1_{m}") for m in range(BLOCKS)]
                 for m in range(BLOCKS):
-                    nc.scalar.activation(x1[m][:], acc1[m][:], RELU, bias=bias[:, m : m + 1])
+                    nc.scalar.activation(x1[m][:], acc1[m][:], RELU, bias=bias1[:, m : m + 1])
                 return x1
 
             def layer2(c, x1):
@@ -100,16 +95,13 @@ def tile_stochasticrewiring_b_kernel(tc, h, hi, w1, b1, w2, b2, offs, out):
                         )
                     result = staged.tile([P, CHUNK], F32, name="result")
                     if r % 2 == 0:
-                        nc.scalar.activation(result[:], acc2[:], RELU, bias=bias[:, BLOCKS + r : BLOCKS + r + 1])
+                        nc.scalar.activation(result[:], acc2[:], RELU, bias=bias2[:, r : r + 1])
                     else:
-                        nc.vector.tensor_scalar(result[:], acc2[:], bias[:, BLOCKS + r : BLOCKS + r + 1], 0.0, ADD, MAX)
+                        nc.vector.tensor_scalar(result[:], acc2[:], bias2[:, r : r + 1], 0.0, ADD, MAX)
                     nc.sync.dma_start(out[r * P : (r + 1) * P, c * CHUNK : (c + 1) * CHUNK], result[:])
 
             feats = [features(0), features(1)]
             acc1 = layer1_products(feats[0])
-            bias_cols = psum.tile([P, CHUNK], F32, name="bias_cols", tag="acc")
-            nc.tensor.transpose(bias_cols[:, 0:P], bias_rows[:], identity[:])
-            nc.scalar.activation(bias[:], bias_cols[:, 0 : 2 * BLOCKS], COPY)
             x1 = [layer1_relu(acc1)]
             for c in range(N_CHUNKS):
                 if c + 2 < N_CHUNKS:

@@ -2,7 +2,11 @@ import concourse.mybir as mybir
 
 F32, BF16, U16 = mybir.dt.float32, mybir.dt.bfloat16, mybir.dt.uint16
 ADD, MULT, MAX = mybir.AluOpType.add, mybir.AluOpType.mult, mybir.AluOpType.max
-COPY, RELU = mybir.ActivationFunctionType.Copy, mybir.ActivationFunctionType.Relu
+COPY, RELU, ABS = (
+    mybir.ActivationFunctionType.Copy,
+    mybir.ActivationFunctionType.Relu,
+    mybir.ActivationFunctionType.Abs,
+)
 
 P = 128
 NODES = 512
@@ -12,7 +16,7 @@ BLOCKS = HID // P
 CHUNK = 512
 N_CHUNKS = EDGES // CHUNK
 FIRST, PICKED, ABSDIFF, PROD = 0, 1, 2, 3
-READY_ORDER = (FIRST, PROD, ABSDIFF, PICKED)
+READY_ORDER = (FIRST, PROD, PICKED, ABSDIFF)
 
 FLOPS = 2 * EDGES * (BLOCKS * P * HID + HID * HID)
 
@@ -28,6 +32,10 @@ def tile_stochasticrewiring_b_kernel(tc, h, hi, w1, b1, w2, b2, offs, out):
     ):
         hi_sb = [held.tile([P, CHUNK], F32, name=f"hi_sb{c}") for c in range(N_CHUNKS)]
         nc.scalar.dma_start(hi_sb[0][:], hi[:, 0:CHUNK])
+        zeros = held.tile([P, 1], F32, name="zeros")
+        nc.gpsimd.memset(zeros[:], 0.0)
+        table_warmer = held.tile([P, 1], F32, name="table_warmer")
+        nc.scalar.activation(table_warmer[:], zeros[:], COPY)
         offsets = held.tile([P, EDGES // 16], U16, name="offsets")
         nc.sync.dma_start(offsets[:], offs)
         h_sb = held.tile([P, NODES], F32, name="h_sb")
@@ -55,14 +63,14 @@ def tile_stochasticrewiring_b_kernel(tc, h, hi, w1, b1, w2, b2, offs, out):
             nc.scalar.activation(neg_first[:], first[:], COPY, scale=-1.0)
             prod = work.tile([P, CHUNK], F32, name="prod")
             nc.vector.tensor_tensor(prod[:], picked_cols, first[:], MULT)
-            prod_bf = feat.tile([P, CHUNK], BF16, name="prod_bf")
-            nc.vector.tensor_copy(prod_bf[:], prod[:])
             diff = work.tile([P, CHUNK], F32, name="diff")
             nc.vector.tensor_tensor(diff[:], picked_cols, neg_first[:], ADD)
-            absdiff_bf = feat.tile([P, CHUNK], BF16, name="absdiff_bf")
-            nc.vector.scalar_tensor_tensor(absdiff_bf[:], diff[:], -1.0, diff[:], MULT, MAX)
+            prod_bf = feat.tile([P, CHUNK], BF16, name="prod_bf")
+            nc.scalar.activation(prod_bf[:], prod[:], COPY)
             picked_bf = feat.tile([P, CHUNK], BF16, name="picked_bf")
             nc.vector.tensor_tensor(picked_bf[:], diff[:], first[:], ADD)
+            absdiff_bf = feat.tile([P, CHUNK], BF16, name="absdiff_bf")
+            nc.scalar.activation(absdiff_bf[:], diff[:], ABS)
             return {FIRST: first_bf, PICKED: picked_bf, ABSDIFF: absdiff_bf, PROD: prod_bf}
 
         with tc.psum_pool(name="psum", bufs=8) as psum:

@@ -26,6 +26,7 @@ def tile_stochasticrewiring_b_kernel(tc, h, hi, w1, b1, w2, b2, offs, out):
     with (
         tc.tile_pool(name="held", bufs=1) as held,
         tc.tile_pool(name="work", bufs=2) as work,
+        tc.tile_pool(name="ahead", bufs=4) as ahead,
         tc.tile_pool(name="feat", bufs=3) as feat,
         tc.tile_pool(name="hidden", bufs=2) as hidden,
         tc.tile_pool(name="staged", bufs=4) as staged,
@@ -54,13 +55,16 @@ def tile_stochasticrewiring_b_kernel(tc, h, hi, w1, b1, w2, b2, offs, out):
         for c in range(2, N_CHUNKS):
             nc.sync.dma_start(hi_sb[c][:], hi[:, c * CHUNK : (c + 1) * CHUNK])
 
-        def features(c):
+        def first_node(c):
+            first_bf = ahead.tile([P, CHUNK], BF16, name="first_bf")
+            nc.scalar.activation(first_bf[:], hi_sb[c][:], COPY)
+            neg_first = ahead.tile([P, CHUNK], F32, name="neg_first")
+            nc.scalar.activation(neg_first[:], hi_sb[c][:], COPY, scale=-1.0)
+            return first_bf, neg_first
+
+        def features(c, first_bf, neg_first):
             first = hi_sb[c]
             picked_cols = h_sb[:].indirect(offsets[:, c * (CHUNK // 16) : (c + 1) * (CHUNK // 16)])
-            first_bf = feat.tile([P, CHUNK], BF16, name="first_bf")
-            nc.scalar.activation(first_bf[:], first[:], COPY)
-            neg_first = work.tile([P, CHUNK], F32, name="neg_first")
-            nc.scalar.activation(neg_first[:], first[:], COPY, scale=-1.0)
             prod = work.tile([P, CHUNK], F32, name="prod")
             nc.vector.tensor_tensor(prod[:], picked_cols, first[:], MULT)
             diff = work.tile([P, CHUNK], F32, name="diff")
@@ -95,25 +99,37 @@ def tile_stochasticrewiring_b_kernel(tc, h, hi, w1, b1, w2, b2, offs, out):
                 return x1
 
             def layer2(c, x1):
-                for r in range(BLOCKS):
+                pieces = [(r, 0, CHUNK) for r in range(BLOCKS)]
+                if c == N_CHUNKS - 1:
+                    pieces = pieces[:-1] + [(BLOCKS - 1, 0, CHUNK // 2), (BLOCKS - 1, CHUNK // 2, CHUNK)]
+                for i, (r, lo, up) in enumerate(pieces):
                     acc2 = psum.tile([P, CHUNK], F32, name="acc2", tag="acc")
                     for k in range(BLOCKS):
                         nc.tensor.matmul(
-                            acc2[:], w2_sb[:, k, r * P : (r + 1) * P], x1[k][:], start=(k == 0), stop=(k == BLOCKS - 1)
+                            acc2[:, lo:up],
+                            w2_sb[:, k, r * P : (r + 1) * P],
+                            x1[k][:, lo:up],
+                            start=(k == 0),
+                            stop=(k == BLOCKS - 1),
                         )
                     result = staged.tile([P, CHUNK], F32, name="result")
-                    if r % 2 == 0:
-                        nc.scalar.activation(result[:], acc2[:], RELU, bias=bias2[:, r : r + 1])
+                    if i % 2 == 0:
+                        nc.scalar.activation(result[:, lo:up], acc2[:, lo:up], RELU, bias=bias2[:, r : r + 1])
                     else:
-                        nc.vector.tensor_scalar(result[:], acc2[:], bias2[:, r : r + 1], 0.0, ADD, MAX)
-                    nc.sync.dma_start(out[r * P : (r + 1) * P, c * CHUNK : (c + 1) * CHUNK], result[:])
+                        nc.vector.tensor_scalar(result[:, lo:up], acc2[:, lo:up], bias2[:, r : r + 1], 0.0, ADD, MAX)
+                    nc.sync.dma_start(out[r * P : (r + 1) * P, c * CHUNK + lo : c * CHUNK + up], result[:, lo:up])
 
-            feats = [features(0), features(1)]
+            firsts = [first_node(0)]
+            feats = [features(0, *firsts[0])]
+            firsts.extend([first_node(1), first_node(2)])
+            feats.append(features(1, *firsts[1]))
             acc1 = layer1_products(feats[0])
             x1 = [layer1_relu(acc1)]
             for c in range(N_CHUNKS):
+                if c + 3 < N_CHUNKS:
+                    firsts.append(first_node(c + 3))
                 if c + 2 < N_CHUNKS:
-                    feats.append(features(c + 2))
+                    feats.append(features(c + 2, *firsts[c + 2]))
                 if c + 1 < N_CHUNKS:
                     x1.append(layer1_relu(layer1_products(feats[c + 1])))
                 layer2(c, x1[c])

@@ -34,7 +34,7 @@ def tile_stochasticrewiring_b_kernel(tc, h, hi, w1, b1, w2, b2, offs, out):
         hi_sb = [held.tile([P, CHUNK], F32, name=f"hi_sb{c}") for c in range(N_CHUNKS)]
         nc.scalar.dma_start(hi_sb[0][:], hi[:, 0:CHUNK])
         zeros = held.tile([P, 1], F32, name="zeros")
-        nc.gpsimd.memset(zeros[:], 0.0)
+        nc.vector.memset(zeros[:], 0.0)
         table_warmer = held.tile([P, 1], F32, name="table_warmer")
         nc.scalar.activation(table_warmer[:], zeros[:], COPY)
         offsets = held.tile([P, EDGES // 16], U16, name="offsets")
@@ -57,7 +57,10 @@ def tile_stochasticrewiring_b_kernel(tc, h, hi, w1, b1, w2, b2, offs, out):
 
         def first_node(c):
             first_bf = ahead.tile([P, CHUNK], BF16, name="first_bf")
-            nc.scalar.activation(first_bf[:], hi_sb[c][:], COPY)
+            if c == 0:
+                nc.vector.tensor_copy(first_bf[:], hi_sb[c][:])
+            else:
+                nc.scalar.activation(first_bf[:], hi_sb[c][:], COPY)
             neg_first = ahead.tile([P, CHUNK], F32, name="neg_first")
             nc.scalar.activation(neg_first[:], hi_sb[c][:], COPY, scale=-1.0)
             return first_bf, neg_first

@@ -32,7 +32,10 @@ def tile_stochasticrewiring_b_kernel(tc, h, hi, w1, b1, w2, b2, offs, out):
         tc.tile_pool(name="staged", bufs=4) as staged,
     ):
         hi_sb = [held.tile([P, CHUNK], F32, name=f"hi_sb{c}") for c in range(N_CHUNKS)]
-        nc.scalar.dma_start(hi_sb[0][:], hi[:, 0:CHUNK])
+        nc.sync.dma_start(hi_sb[0][:], hi[:, 0:CHUNK])
+        w1_sb = held.tile([P, BLOCKS, HID], BF16, name="w1_sb")
+        w1_blocks = w1.rearrange("(k p) m -> p k m", p=P)
+        nc.sync.dma_start(w1_sb[:, 0:1, :], w1_blocks[:, 0:1, :])
         zeros = held.tile([P, 1], F32, name="zeros")
         nc.vector.memset(zeros[:], 0.0)
         table_warmer = held.tile([P, 1], F32, name="table_warmer")
@@ -41,9 +44,6 @@ def tile_stochasticrewiring_b_kernel(tc, h, hi, w1, b1, w2, b2, offs, out):
         nc.sync.dma_start(offsets[:], offs)
         h_sb = held.tile([P, NODES], F32, name="h_sb")
         nc.sync.dma_start(h_sb[:], h)
-        w1_sb = held.tile([P, BLOCKS, HID], BF16, name="w1_sb")
-        w1_blocks = w1.rearrange("(k p) m -> p k m", p=P)
-        nc.sync.dma_start(w1_sb[:, 0:1, :], w1_blocks[:, 0:1, :])
         nc.sync.dma_start(w1_sb[:, 1:BLOCKS, :], w1_blocks[:, 1:BLOCKS, :])
         nc.sync.dma_start(hi_sb[1][:], hi[:, CHUNK : 2 * CHUNK])
         bias1 = held.tile([P, BLOCKS], F32, name="bias1")

@@ -44,8 +44,8 @@ def tile_stochasticrewiring_b_kernel(tc, h, hi, w1, b1, w2, b2, offs, out):
         nc.sync.dma_start(offsets[:], offs)
         h_sb = held.tile([P, NODES], F32, name="h_sb")
         nc.sync.dma_start(h_sb[:], h)
-        nc.sync.dma_start(w1_sb[:, 1:BLOCKS, :], w1_blocks[:, 1:BLOCKS, :])
         nc.sync.dma_start(hi_sb[1][:], hi[:, CHUNK : 2 * CHUNK])
+        nc.sync.dma_start(w1_sb[:, 1:BLOCKS, :], w1_blocks[:, 1:BLOCKS, :])
         bias1 = held.tile([P, BLOCKS], F32, name="bias1")
         nc.sync.dma_start(bias1[:], b1.rearrange("(m p) o -> p (m o)", p=P))
         bias2 = held.tile([P, BLOCKS], F32, name="bias2")
@@ -82,9 +82,8 @@ def tile_stochasticrewiring_b_kernel(tc, h, hi, w1, b1, w2, b2, offs, out):
 
         with tc.psum_pool(name="psum", bufs=8) as psum:
 
-            def layer1_products(feats):
-                acc1 = [psum.tile([P, CHUNK], F32, name=f"acc1_{m}", tag="acc") for m in range(BLOCKS)]
-                for k in READY_ORDER:
+            def layer1_products(acc1, feats, blocks):
+                for k in blocks:
                     for m in range(BLOCKS):
                         nc.tensor.matmul(
                             acc1[m][:],
@@ -93,6 +92,10 @@ def tile_stochasticrewiring_b_kernel(tc, h, hi, w1, b1, w2, b2, offs, out):
                             start=(k == READY_ORDER[0]),
                             stop=(k == READY_ORDER[-1]),
                         )
+
+            def layer1_open(feats):
+                acc1 = [psum.tile([P, CHUNK], F32, name=f"acc1_{m}", tag="acc") for m in range(BLOCKS)]
+                layer1_products(acc1, feats, READY_ORDER[:1])
                 return acc1
 
             def layer1_relu(acc1):
@@ -122,17 +125,21 @@ def tile_stochasticrewiring_b_kernel(tc, h, hi, w1, b1, w2, b2, offs, out):
                         nc.vector.tensor_scalar(result[:, lo:up], acc2[:, lo:up], bias2[:, r : r + 1], 0.0, ADD, MAX)
                     nc.sync.dma_start(out[r * P : (r + 1) * P, c * CHUNK + lo : c * CHUNK + up], result[:, lo:up])
 
-            firsts = [first_node(0)]
+            firsts = [first_node(0), first_node(1)]
+            acc1 = [layer1_open({FIRST: firsts[c][0]}) for c in range(2)]
             feats = [features(0, *firsts[0])]
-            firsts.extend([first_node(1), first_node(2)])
+            firsts.append(first_node(2))
             feats.append(features(1, *firsts[1]))
-            acc1 = layer1_products(feats[0])
-            x1 = [layer1_relu(acc1)]
+            layer1_products(acc1[0], feats[0], READY_ORDER[1:])
+            x1 = [layer1_relu(acc1[0])]
             for c in range(N_CHUNKS):
                 if c + 3 < N_CHUNKS:
                     firsts.append(first_node(c + 3))
                 if c + 2 < N_CHUNKS:
                     feats.append(features(c + 2, *firsts[c + 2]))
                 if c + 1 < N_CHUNKS:
-                    x1.append(layer1_relu(layer1_products(feats[c + 1])))
+                    if c + 1 == len(acc1):
+                        acc1.append(layer1_open(feats[c + 1]))
+                    layer1_products(acc1[c + 1], feats[c + 1], READY_ORDER[1:])
+                    x1.append(layer1_relu(acc1[c + 1]))
                 layer2(c, x1[c])

import concourse.mybir as mybir

F32, BF16, U16 = mybir.dt.float32, mybir.dt.bfloat16, mybir.dt.uint16
ADD, MULT, MAX = mybir.AluOpType.add, mybir.AluOpType.mult, mybir.AluOpType.max
COPY, RELU, ABS = (
    mybir.ActivationFunctionType.Copy,
    mybir.ActivationFunctionType.Relu,
    mybir.ActivationFunctionType.Abs,
)

P = 128
NODES = 512
EDGES = 4096
HID = 512
BLOCKS = HID // P
CHUNK = 512
N_CHUNKS = EDGES // CHUNK
FIRST, PICKED, ABSDIFF, PROD = 0, 1, 2, 3
READY_ORDER = (FIRST, PROD, PICKED, ABSDIFF)

FLOPS = 2 * EDGES * (BLOCKS * P * HID + HID * HID)


def tile_stochasticrewiring_b_kernel(tc, h, hi, w1, b1, w2, b2, offs, out):
    nc = tc.nc
    with (
        tc.tile_pool(name="held", bufs=1) as held,
        tc.tile_pool(name="work", bufs=2) as work,
        tc.tile_pool(name="ahead", bufs=4) as ahead,
        tc.tile_pool(name="feat", bufs=3) as feat,
        tc.tile_pool(name="hidden", bufs=2) as hidden,
        tc.tile_pool(name="staged", bufs=4) as staged,
    ):
        hi_sb = [held.tile([P, CHUNK], F32, name=f"hi_sb{c}") for c in range(N_CHUNKS)]
        nc.sync.dma_start(hi_sb[0][:], hi[:, 0:CHUNK])
        w1_sb = held.tile([P, BLOCKS, HID], BF16, name="w1_sb")
        w1_blocks = w1.rearrange("(k p) m -> p k m", p=P)
        nc.sync.dma_start(w1_sb[:, 0:1, :], w1_blocks[:, 0:1, :])
        zeros = held.tile([P, 1], F32, name="zeros")
        nc.vector.memset(zeros[:], 0.0)
        table_warmer = held.tile([P, 1], F32, name="table_warmer")
        nc.scalar.activation(table_warmer[:], zeros[:], COPY)
        offsets = held.tile([P, EDGES // 16], U16, name="offsets")
        nc.sync.dma_start(offsets[:], offs)
        h_sb = held.tile([P, NODES], F32, name="h_sb")
        nc.sync.dma_start(h_sb[:], h)
        nc.sync.dma_start(hi_sb[1][:], hi[:, CHUNK : 2 * CHUNK])
        nc.sync.dma_start(w1_sb[:, 1:BLOCKS, :], w1_blocks[:, 1:BLOCKS, :])
        bias1 = held.tile([P, BLOCKS], F32, name="bias1")
        nc.sync.dma_start(bias1[:], b1.rearrange("(m p) o -> p (m o)", p=P))
        bias2 = held.tile([P, BLOCKS], F32, name="bias2")
        nc.sync.dma_start(bias2[:], b2.rearrange("(m p) o -> p (m o)", p=P))
        w2_sb = held.tile([P, BLOCKS, HID], BF16, name="w2_sb")
        nc.sync.dma_start(w2_sb[:], w2.rearrange("(k p) m -> p k m", p=P))
        for c in range(2, N_CHUNKS):
            nc.sync.dma_start(hi_sb[c][:], hi[:, c * CHUNK : (c + 1) * CHUNK])

        def first_node(c):
            first_bf = ahead.tile([P, CHUNK], BF16, name="first_bf")
            if c == 0:
                nc.vector.tensor_copy(first_bf[:], hi_sb[c][:])
            else:
                nc.scalar.activation(first_bf[:], hi_sb[c][:], COPY)
            neg_first = ahead.tile([P, CHUNK], F32, name="neg_first")
            nc.scalar.activation(neg_first[:], hi_sb[c][:], COPY, scale=-1.0)
            return first_bf, neg_first

        def features(c, first_bf, neg_first):
            first = hi_sb[c]
            picked_cols = h_sb[:].indirect(offsets[:, c * (CHUNK // 16) : (c + 1) * (CHUNK // 16)])
            prod = work.tile([P, CHUNK], F32, name="prod")
            nc.vector.tensor_tensor(prod[:], picked_cols, first[:], MULT)
            diff = work.tile([P, CHUNK], F32, name="diff")
            nc.vector.tensor_tensor(diff[:], picked_cols, neg_first[:], ADD)
            prod_bf = feat.tile([P, CHUNK], BF16, name="prod_bf")
            nc.scalar.activation(prod_bf[:], prod[:], COPY)
            picked_bf = feat.tile([P, CHUNK], BF16, name="picked_bf")
            nc.vector.tensor_tensor(picked_bf[:], diff[:], first[:], ADD)
            absdiff_bf = feat.tile([P, CHUNK], BF16, name="absdiff_bf")
            nc.scalar.activation(absdiff_bf[:], diff[:], ABS)
            return {FIRST: first_bf, PICKED: picked_bf, ABSDIFF: absdiff_bf, PROD: prod_bf}

        with tc.psum_pool(name="psum", bufs=8) as psum:

            def layer1_products(acc1, feats, blocks):
                for k in blocks:
                    for m in range(BLOCKS):
                        nc.tensor.matmul(
                            acc1[m][:],
                            w1_sb[:, k, m * P : (m + 1) * P],
                            feats[k][:],
                            start=(k == READY_ORDER[0]),
                            stop=(k == READY_ORDER[-1]),
                        )

            def layer1_open(feats):
                acc1 = [psum.tile([P, CHUNK], F32, name=f"acc1_{m}", tag="acc") for m in range(BLOCKS)]
                layer1_products(acc1, feats, READY_ORDER[:1])
                return acc1

            def layer1_relu(acc1):
                x1 = [hidden.tile([P, CHUNK], BF16, name=f"x1_{m}") for m in range(BLOCKS)]
                for m in range(BLOCKS):
                    nc.scalar.activation(x1[m][:], acc1[m][:], RELU, bias=bias1[:, m : m + 1])
                return x1

            def layer2(c, x1):
                pieces = [(r, 0, CHUNK) for r in range(BLOCKS)]
                if c == N_CHUNKS - 1:
                    pieces = pieces[:-1] + [(BLOCKS - 1, 0, CHUNK // 2), (BLOCKS - 1, CHUNK // 2, CHUNK)]
                for i, (r, lo, up) in enumerate(pieces):
                    acc2 = psum.tile([P, CHUNK], F32, name="acc2", tag="acc")
                    for k in range(BLOCKS):
                        nc.tensor.matmul(
                            acc2[:, lo:up],
                            w2_sb[:, k, r * P : (r + 1) * P],
                            x1[k][:, lo:up],
                            start=(k == 0),
                            stop=(k == BLOCKS - 1),
                        )
                    result = staged.tile([P, CHUNK], F32, name="result")
                    if i % 2 == 0:
                        nc.scalar.activation(result[:, lo:up], acc2[:, lo:up], RELU, bias=bias2[:, r : r + 1])
                    else:
                        nc.vector.tensor_scalar(result[:, lo:up], acc2[:, lo:up], bias2[:, r : r + 1], 0.0, ADD, MAX)
                    nc.sync.dma_start(out[r * P : (r + 1) * P, c * CHUNK + lo : c * CHUNK + up], result[:, lo:up])

            firsts = [first_node(0), first_node(1)]
            acc1 = [layer1_open({FIRST: firsts[c][0]}) for c in range(2)]
            feats = [features(0, *firsts[0])]
            firsts.append(first_node(2))
            feats.append(features(1, *firsts[1]))
            layer1_products(acc1[0], feats[0], READY_ORDER[1:])
            x1 = [layer1_relu(acc1[0])]
            for c in range(N_CHUNKS):
                if c + 3 < N_CHUNKS:
                    firsts.append(first_node(c + 3))
                if c + 2 < N_CHUNKS:
                    feats.append(features(c + 2, *firsts[c + 2]))
                if c + 1 < N_CHUNKS:
                    if c + 1 == len(acc1):
                        acc1.append(layer1_open(feats[c + 1]))
                    layer1_products(acc1[c + 1], feats[c + 1], READY_ORDER[1:])
                    x1.append(layer1_relu(acc1[c + 1]))
                layer2(c, x1[c])
